import numpy as np
import ml_dtypes


def mxq(x, axis, fmt="e4m3"):
    dtype, down = {"e4m3": (ml_dtypes.float8_e4m3fn, 7), "e5m2": (ml_dtypes.float8_e5m2, 14)}[fmt]
    v = np.moveaxis(np.asarray(x, np.float32).astype(ml_dtypes.bfloat16).astype(np.float64), axis, -1)
    blocks = v.reshape(v.shape[:-1] + (-1, 32))
    amax = np.abs(blocks).max(-1, keepdims=True)
    byte = np.maximum(np.where(amax > 0, np.frexp(amax)[1] - 1 + 127, 0) - down, 1)
    scale = np.exp2(byte - 127.0)
    codes = (blocks / scale).astype(np.float32).astype(dtype).astype(np.float64)
    return np.moveaxis((codes * scale).reshape(v.shape), -1, axis)


WIDE = False


def mx_kscale(k):
    if not WIDE:
        return np.ones(k)
    levels = np.array([10, -10, 5, -5, 0])
    if k % 512:
        return np.exp2(np.random.permutation(np.resize(levels, k // 32))).repeat(32)
    a = np.empty((k // 512, 16))
    for p in range(k // 512):
        a[p, :8] = np.random.permutation(np.resize(levels, 8))
        for g in range(8):
            far = levels[np.abs(levels - a[p, g]) >= 10]
            a[p, g + 8] = far[np.random.randint(len(far))]
    return np.exp2(a.ravel()).repeat(32)


BF16 = ml_dtypes.bfloat16


def bf(x):
    return np.asarray(x, np.float32).astype(BF16)


def f64(x):
    return np.asarray(x).astype(np.float64)


B, N, D, H = 128, 17, 2048, 32
D2 = D // 2
D4 = D // 4
EPS = 1e-5


def layernorm(z, g, b):
    mu = z.mean(-1, keepdims=True)
    var = z.var(-1, keepdims=True)
    return (z - mu) / np.sqrt(var + EPS) * g + b


def setup_inputs():
    s, t = mx_kscale(D), mx_kscale(D2)
    r = np.random.standard_normal
    return {"query": bf(r((B, N, D)) * s),
            "A1W": bf(r((D, D2)) / np.sqrt(D) / s[:, None]),
            "A1b": bf(r(D2) * 0.2),
            "g1": bf((1.0 + 0.1 * r(D2)) * t),
            "b1": bf(r(D2) * 0.2 * t),
            "A2W": bf(r((D2, D4)) / np.sqrt(D2) / t[:, None]),
            "A2b": bf(r(D4) * 0.2),
            "g2": bf(1.0 + 0.1 * r(D4)),
            "b2": bf(r(D4) * 0.2)}


def reference(query, A1W, A1b, g1, b1, A2W, A2b, g2, b2):
    u = (mxq(f64(query), 2, "e4m3") @ mxq(f64(A1W), 0, "e4m3")) + f64(A1b)
    j1 = np.maximum(layernorm(u, f64(g1), f64(b1)), 0.0)
    w = (mxq(j1, 2, "e4m3") @ mxq(f64(A2W), 0, "e4m3")) + f64(A2b)
    return np.maximum(layernorm(w, f64(g2), f64(b2)), 0.0)

@@ -1,0 +1,425 @@
+from contextlib import ExitStack
+
+import concourse.mybir as mybir
+from concourse.masks import make_identity
+
+F32 = mybir.dt.float32
+BF16 = mybir.dt.bfloat16
+U32 = mybir.dt.uint32
+U8 = mybir.dt.uint8
+FP8X4 = mybir.dt.float8_e4m3fn_x4
+ALU = mybir.AluOpType
+ACT = mybir.ActivationFunctionType
+
+P = 128
+PACK = 4
+K_PASS = P * PACK
+BANK = 512
+
+TOKENS = 128 * 17
+D = 2048
+D2 = 1024
+D4 = 512
+EPS = 1e-5
+TILES = TOKENS // P
+PASSES1 = D // K_PASS
+PASSES2 = D2 // K_PASS
+HALVES1 = D2 // BANK
+
+FLOPS = 2 * TOKENS * (D * D2 + D2 * D4)
+
+Q_BUFS = 8
+W1_PERIOD = -1
+W2_REGROUP_PERIOD = -1
+W2_QUANTISE_PERIOD = 1
+
+
+def tile_multiheadedattention_pa_kernel(tc, query, A1W, A1b, g1, b1, A2W, A2b, g2, b2, out):
+    nc = tc.nc
+    q_rows = query.flatten_outer_dims()
+    out_rows = out.flatten_outer_dims()
+    w1_view = A1W.rearrange("(g p t) n -> g p t n", g=PASSES1, p=P, t=PACK)
+    w2_view = A2W.rearrange("(c p t) n -> c p t n", c=PASSES2, p=P, t=PACK)
+    g1_view = g1.rearrange("(c p t) -> p c t", c=PASSES2, p=P, t=PACK)
+    b1_view = b1.rearrange("(c p t) -> p c t", c=PASSES2, p=P, t=PACK)
+
+    with ExitStack() as ctx:
+        keep = ctx.enter_context(tc.tile_pool(name="keep", bufs=1))
+        q_pool = ctx.enter_context(tc.tile_pool(name="q_pool", bufs=Q_BUFS))
+        w_pool = ctx.enter_context(tc.tile_pool(name="w_pool", bufs=2))
+        work = ctx.enter_context(tc.tile_pool(name="work", bufs=2))
+        small = ctx.enter_context(tc.tile_pool(name="small", bufs=4))
+        psum = ctx.enter_context(tc.psum_pool(name="psum", bufs=2))
+        ctx.enter_context(tc.manual_schedule())
+
+        ident = keep.tile([P, P], F32)
+        make_identity(nc, ident[:])
+        eps = keep.tile([P, 1], F32)
+        nc.vector.memset(eps[:], EPS)
+        table_warm = keep.tile([P, 1], F32)
+        nc.scalar.activation(out=table_warm[:], in_=eps[:], func=ACT.Abs_reciprocal_sqrt)
+
+
+        q_tiles = {}
+        w1_raw = {}
+        w2_raw = {}
+
+        def load_query(i):
+            q_sb = q_pool.tile([P, D], BF16)
+            nc.sync.dma_start(out=q_sb[:], in_=q_rows[i * P : (i + 1) * P, :])
+            q_tiles[i] = q_sb
+
+        def load_w1(g):
+            raw1 = keep.tile([P, PACK, D2], BF16, name="raw1_%d" % g)
+            nc.sync.dma_start(out=raw1[:], in_=w1_view[g])
+            w1_raw[g] = raw1
+
+        def load_w2(c):
+            raw2 = keep.tile([P, PACK, D4], BF16, name="raw2_%d" % c)
+            nc.sync.dma_start(out=raw2[:], in_=w2_view[c])
+            w2_raw[c] = raw2
+
+        def load_row_to_all_partitions(vec, width, name):
+            spread = keep.tile([P, width], BF16, name=name)
+            nc.sync.dma_start(out=spread[:], in_=vec.partition_broadcast(P))
+            return spread
+
+        load_query(0)
+        for g in range(PASSES1):
+            load_w1(g)
+        a1_all = load_row_to_all_partitions(A1b, D2, "a1_all")
+        load_query(1)
+        for c in range(PASSES2):
+            load_w2(c)
+        g1_raw = keep.tile([P, PASSES2, PACK], BF16)
+        nc.sync.dma_start(out=g1_raw[:], in_=g1_view)
+        b1_raw = keep.tile([P, PASSES2, PACK], BF16)
+        nc.sync.dma_start(out=b1_raw[:], in_=b1_view)
+        load_query(2)
+        load_query(3)
+        a2_all = load_row_to_all_partitions(A2b, D4, "a2_all")
+        g2_all = load_row_to_all_partitions(g2, D4, "g2_all")
+        b2_all = load_row_to_all_partitions(b2, D4, "b2_all")
+        for i in range(4, Q_BUFS):
+            load_query(i)
+
+        gb = keep.tile([P, 2 * D2 // P], F32)
+        a1_perm = keep.tile([P, HALVES1, PACK, P], BF16)
+
+        w1_codes = keep.tile([P, PASSES1, D2], U32, align_bytes=64)
+        w1_scales = keep.tile([P, PASSES1, D2], U8, align_bytes=64)
+        w2_codes = keep.tile([P, PASSES2, D4], U32, align_bytes=64)
+        w2_scales = keep.tile([P, PASSES2, D4], U8, align_bytes=64)
+        w2_grouped = {}
+
+        def regroup(copy, dst, src):
+            copy(
+                out=dst.rearrange("p (c i) t -> p c t i", i=4),
+                in_=src.rearrange("p t (c i) -> p c t i", i=4),
+            )
+
+        w1_grouped = {}
+
+        def regroup_w1(g):
+            rows = w1_raw[g][:]
+            by_scalar = w_pool.tile([P, BANK, PACK], BF16, align_bytes=64)
+            regroup(nc.scalar.copy, by_scalar[:], rows[:, :, BANK : 2 * BANK])
+            by_vector = w_pool.tile([P, BANK, PACK], BF16, align_bytes=64)
+            regroup(nc.vector.tensor_copy, by_vector[:], rows[:, :, 0:BANK])
+            w1_grouped[g] = (by_vector, by_scalar)
+
+        def quantise_w1(g, h):
+            cols = slice(h * BANK, (h + 1) * BANK)
+            nc.vector.quantize_mx(
+                out=w1_codes[:, g, cols].bitcast(FP8X4),
+                scales=w1_scales[:, g, cols],
+                in_=w1_grouped[g][h][:].rearrange("p n t -> p (n t)"),
+            )
+
+        def prepare_w1(g):
+            regroup_w1(g)
+            if g > 0:
+                quantise_w1(g - 1, 1)
+            quantise_w1(g, 0)
+
+        def regroup_w2(c):
+            grouped2 = keep.tile([P, D4, PACK], BF16, align_bytes=64, name="grouped2_%d" % c)
+            regroup(nc.scalar.copy, grouped2[:], w2_raw[c][:])
+            w2_grouped[c] = grouped2
+
+        def quantise_w2(c):
+            nc.vector.quantize_mx(
+                out=w2_codes[:, c, :].bitcast(FP8X4),
+                scales=w2_scales[:, c, :],
+                in_=w2_grouped[c][:].rearrange("p n t -> p (n t)"),
+            )
+
+        q_banks = {}
+        q_grouped = {}
+        q_codes = {}
+        q_scales = {}
+        u_banks = {}
+        u_tiles = {}
+        stats1 = {}
+        z_tiles = {}
+        z_banks = {}
+        j_planes = {}
+        j_grouped = {}
+        j_codes = {}
+        j_scales = {}
+        w_banks = {}
+        w_tiles = {}
+        stats2 = {}
+        y_tiles = {}
+
+        def transpose_query(i):
+            words = q_tiles[i][:].bitcast(F32)
+            q_banks[i] = []
+            for b in range(2):
+                qt = psum.tile([P, 2, 2, P], F32)
+                for gg in range(2):
+                    for u in range(2):
+                        first = 256 * (2 * b + gg)
+                        nc.tensor.transpose(qt[:, gg, u, :], words[:, first + u : first + 256 : 2], ident[:])
+                q_banks[i].append(qt)
+
+        def query_out_of_psum(i):
+            qg = work.tile([P, PASSES1 * P * PACK], BF16, align_bytes=64)
+            qg_words = qg[:].bitcast(F32).rearrange("p (g n u) -> p g n u", g=PASSES1, u=2)
+            for b in range(2):
+                nc.scalar.copy(
+                    out=qg_words[:, 2 * b : 2 * b + 2, :, :],
+                    in_=q_banks[i][b][:].rearrange("p g u n -> p g n u"),
+                )
+            q_grouped[i] = qg
+
+        def quantise_query(i):
+            qc = work.tile([P, PASSES1 * P], U32, align_bytes=64, bufs=3)
+            qs = work.tile([P, PASSES1 * P], U8, align_bytes=64, bufs=3)
+            nc.vector.quantize_mx(out=qc[:].bitcast(FP8X4), scales=qs[:], in_=q_grouped[i][:])
+            q_codes[i] = qc
+            q_scales[i] = qs
+
+        def first_product(i, h):
+            cols = slice(h * BANK, (h + 1) * BANK)
+            acc1 = psum.tile([P, BANK], F32)
+            for g in range(PASSES1):
+                toks = slice(g * P, (g + 1) * P)
+                nc.tensor.matmul_mx(
+                    out=acc1[:],
+                    lhsT=q_codes[i][:, toks].bitcast(FP8X4),
+                    lhsT_scale=q_scales[i][:, toks],
+                    rhs=w1_codes[:, g, cols].bitcast(FP8X4),
+                    rhs_scale=w1_scales[:, g, cols],
+                    start=(g == 0),
+                    stop=(g == PASSES1 - 1),
+                )
+            u_banks[i, h] = acc1
+
+        def add_bias1(i):
+            u = work.tile([P, D2], F32)
+            row_sum = small.tile([P, HALVES1], F32)
+            for h in range(HALVES1):
+                cols = slice(h * BANK, (h + 1) * BANK)
+                nc.vector.scalar_tensor_tensor(
+                    out=u[:, cols].rearrange("p (t m) -> p t m", t=PACK),
+                    in0=u_banks[i, h][:].rearrange("p (m t) -> p t m", t=PACK),
+                    scalar=1.0, in1=a1_perm[:, h, :, :],
+                    op0=ALU.mult, op1=ALU.add, accum_out=row_sum[:, h : h + 1],
+                )
+            u_tiles[i] = u
+            stats1[i] = {"row_sum": row_sum}
+
+        def mean1(i):
+            row_sum = stats1[i]["row_sum"]
+            neg_mean = small.tile([P, 1], F32)
+            nc.vector.tensor_scalar(
+                out=neg_mean[:], in0=row_sum[:, 0:1], scalar1=row_sum[:, 1:2], scalar2=-1.0 / D2,
+                op0=ALU.add, op1=ALU.mult,
+            )
+            stats1[i]["neg_mean"] = neg_mean
+
+        def deviation1(i):
+            squares = work.tile([P, D2], F32)
+            sq_sum = small.tile([P, 1], F32)
+            nc.scalar.activation(
+                out=squares[:], in_=u_tiles[i][:], func=ACT.Square,
+                bias=stats1[i]["neg_mean"][:], scale=1.0, accum_out=sq_sum[:],
+            )
+            stats1[i]["sq_sum"] = sq_sum
+
+        def inverse_deviation1(i):
+            rstd = small.tile([P, 1], F32)
+            nc.scalar.activation(
+                out=rstd[:], in_=stats1[i]["sq_sum"][:], func=ACT.Abs_reciprocal_sqrt,
+                bias=eps[:], scale=1.0 / D2,
+            )
+            stats1[i]["rstd"] = rstd
+
+        def normalise1(i):
+            z = work.tile([P, D2], F32)
+            nc.vector.tensor_scalar(
+                out=z[:], in0=u_tiles[i][:], scalar1=stats1[i]["neg_mean"][:], scalar2=stats1[i]["rstd"][:],
+                op0=ALU.add, op1=ALU.mult,
+            )
+            z_tiles[i] = z
+
+        def transpose_z(i):
+            z_banks[i] = []
+            for c in range(PASSES2):
+                zt = psum.tile([P, PACK, P], F32)
+                for t in range(PACK):
+                    first = K_PASS * c + P * t
+                    nc.tensor.transpose(zt[:, t, :], z_tiles[i][:, first : first + P], ident[:])
+                z_banks[i].append(zt)
+
+        def gain_shift_relu1(i):
+            planes = work.tile([P, PACK, PASSES2, P], BF16)
+            for c in range(PASSES2):
+                for t in range(PACK):
+                    j = PACK * c + t
+                    nc.scalar.activation(
+                        out=planes[:, t, c, :], in_=z_banks[i][c][:, t, :], func=ACT.Relu,
+                        scale=gb[:, j : j + 1], bias=gb[:, D2 // P + j : D2 // P + j + 1],
+                    )
+            j_planes[i] = planes
+
+        def regroup_j1(i):
+            jg = work.tile([P, PASSES2 * P, PACK], BF16, align_bytes=64)
+            regroup(nc.vector.tensor_copy, jg[:], j_planes[i][:].rearrange("p t c n -> p t (c n)"))
+            j_grouped[i] = jg
+
+        def quantise_j1(i):
+            jc = work.tile([P, PASSES2 * P], U32, align_bytes=64)
+            js = work.tile([P, PASSES2 * P], U8, align_bytes=64)
+            nc.vector.quantize_mx(
+                out=jc[:].bitcast(FP8X4), scales=js[:],
+                in_=j_grouped[i][:].rearrange("p n t -> p (n t)"),
+            )
+            j_codes[i] = jc
+            j_scales[i] = js
+
+        def second_product(i):
+            acc2 = psum.tile([P, BANK], F32)
+            for c in range(PASSES2):
+                toks = slice(c * P, (c + 1) * P)
+                nc.tensor.matmul_mx(
+                    out=acc2[:],
+                    lhsT=j_codes[i][:, toks].bitcast(FP8X4),
+                    lhsT_scale=j_scales[i][:, toks],
+                    rhs=w2_codes[:, c, :].bitcast(FP8X4),
+                    rhs_scale=w2_scales[:, c, :],
+                    start=(c == 0),
+                    stop=(c == PASSES2 - 1),
+                )
+            w_banks[i] = acc2
+
+        def add_bias2(i):
+            w = work.tile([P, D4], F32, bufs=3)
+            row_sum2 = small.tile([P, 1], F32)
+            nc.vector.scalar_tensor_tensor(
+                out=w[:], in0=w_banks[i][:], scalar=1.0, in1=a2_all[:],
+                op0=ALU.mult, op1=ALU.add, accum_out=row_sum2[:],
+            )
+            w_tiles[i] = w
+            stats2[i] = {"row_sum": row_sum2}
+
+        def mean2(i):
+            neg_mean2 = small.tile([P, 1], F32)
+            nc.vector.tensor_scalar(
+                out=neg_mean2[:], in0=stats2[i]["row_sum"][:], scalar1=-1.0 / D4, scalar2=None,
+                op0=ALU.mult,
+            )
+            stats2[i]["neg_mean"] = neg_mean2
+
+        def deviation2(i):
+            squares2 = work.tile([P, D4], F32)
+            sq_sum2 = small.tile([P, 1], F32)
+            nc.scalar.activation(
+                out=squares2[:], in_=w_tiles[i][:], func=ACT.Square,
+                bias=stats2[i]["neg_mean"][:], scale=1.0, accum_out=sq_sum2[:],
+            )
+            stats2[i]["sq_sum"] = sq_sum2
+
+        def inverse_deviation2(i):
+            rstd2 = small.tile([P, 1], F32)
+            nc.scalar.activation(
+                out=rstd2[:], in_=stats2[i]["sq_sum"][:], func=ACT.Abs_reciprocal_sqrt,
+                bias=eps[:], scale=1.0 / D4,
+            )
+            stats2[i]["rstd"] = rstd2
+
+        x_tiles = {}
+
+        def centre_gain2(i):
+            x = work.tile([P, D4], F32)
+            nc.vector.scalar_tensor_tensor(
+                out=x[:], in0=w_tiles[i][:], scalar=stats2[i]["neg_mean"][:], in1=g2_all[:],
+                op0=ALU.add, op1=ALU.mult,
+            )
+            x_tiles[i] = x
+
+        def scale_shift2(i):
+            y = work.tile([P, D4], F32)
+            nc.vector.scalar_tensor_tensor(
+                out=y[:], in0=x_tiles[i][:], scalar=stats2[i]["rstd"][:], in1=b2_all[:],
+                op0=ALU.mult, op1=ALU.add,
+            )
+            y_tiles[i] = y
+
+        def relu_and_store(i):
+            result = work.tile([P, D4], F32, bufs=3)
+            nc.scalar.activation(out=result[:], in_=y_tiles[i][:], func=ACT.Relu)
+            nc.sync.dma_start(out=out_rows[i * P : (i + 1) * P, :], in_=result[:])
+
+        def run(step, i, *more):
+            if 0 <= i < TILES:
+                step(i, *more)
+
+        def period(i):
+            if Q_BUFS <= i + 1 + Q_BUFS < TILES:
+                load_query(i + 1 + Q_BUFS)
+            run(first_product, i, 0)
+            run(transpose_query, i + 2)
+            run(first_product, i, 1)
+            run(transpose_z, i - 2)
+            run(regroup_j1, i - 3)
+            run(mean2, i - 4)
+            run(quantise_query, i + 1)
+            if i == W1_PERIOD:
+                for g in range(PASSES1):
+                    prepare_w1(g)
+                quantise_w1(PASSES1 - 1, 1)
+                nc.vector.tensor_copy(
+                    out=gb[:, 0 : D2 // P], in_=g1_raw[:].rearrange("p c t -> p (c t)")
+                )
+                nc.vector.tensor_copy(
+                    out=gb[:, D2 // P : 2 * D2 // P], in_=b1_raw[:].rearrange("p c t -> p (c t)")
+                )
+                nc.vector.tensor_copy(
+                    out=a1_perm[:], in_=a1_all[:].rearrange("p (c m t) -> p c t m", c=HALVES1, t=PACK),
+                )
+            run(quantise_j1, i - 3)
+            run(centre_gain2, i - 4)
+            run(second_product, i - 3)
+            run(deviation1, i - 1)
+            run(deviation2, i - 4)
+            run(query_out_of_psum, i + 2)
+            if i == W2_REGROUP_PERIOD:
+                for c in range(PASSES2):
+                    regroup_w2(c)
+            run(inverse_deviation1, i - 1)
+            run(inverse_deviation2, i - 4)
+            run(gain_shift_relu1, i - 2)
+            run(relu_and_store, i - 5)
+            run(add_bias1, i)
+            run(normalise1, i - 1)
+            run(scale_shift2, i - 4)
+            run(mean1, i)
+            run(add_bias2, i - 3)
+            if i == W2_QUANTISE_PERIOD:
+                for c in range(PASSES2):
+                    quantise_w2(c)
+
+        for i in range(-2, TILES + 5):
+            period(i)

@@ -29,9 +29,6 @@ HALVES1 = D2 // BANK
 FLOPS = 2 * TOKENS * (D * D2 + D2 * D4)
 
 Q_BUFS = 8
-W1_PERIOD = -1
-W2_REGROUP_PERIOD = -1
-W2_QUANTISE_PERIOD = 1
 
 
 def tile_multiheadedattention_pa_kernel(tc, query, A1W, A1b, g1, b1, A2W, A2b, g2, b2, out):
@@ -48,8 +45,8 @@ def tile_multiheadedattention_pa_kernel(tc, query, A1W, A1b, g1, b1, A2W, A2b, g
         q_pool = ctx.enter_context(tc.tile_pool(name="q_pool", bufs=Q_BUFS))
         w_pool = ctx.enter_context(tc.tile_pool(name="w_pool", bufs=2))
         work = ctx.enter_context(tc.tile_pool(name="work", bufs=2))
-        small = ctx.enter_context(tc.tile_pool(name="small", bufs=4))
-        psum = ctx.enter_context(tc.psum_pool(name="psum", bufs=2))
+        small = ctx.enter_context(tc.tile_pool(name="small", bufs=8))
+        psum = ctx.enter_context(tc.psum_pool(name="psum", bufs=4))
         ctx.enter_context(tc.manual_schedule())
 
         ident = keep.tile([P, P], F32)
@@ -85,17 +82,19 @@ def tile_multiheadedattention_pa_kernel(tc, query, A1W, A1b, g1, b1, A2W, A2b, g
             return spread
 
         load_query(0)
-        for g in range(PASSES1):
-            load_w1(g)
+        load_w1(0)
+        load_w1(1)
         a1_all = load_row_to_all_partitions(A1b, D2, "a1_all")
+        load_w1(2)
+        load_w1(3)
         load_query(1)
-        for c in range(PASSES2):
-            load_w2(c)
         g1_raw = keep.tile([P, PASSES2, PACK], BF16)
         nc.sync.dma_start(out=g1_raw[:], in_=g1_view)
         b1_raw = keep.tile([P, PASSES2, PACK], BF16)
         nc.sync.dma_start(out=b1_raw[:], in_=b1_view)
         load_query(2)
+        for c in range(PASSES2):
+            load_w2(c)
         load_query(3)
         a2_all = load_row_to_all_partitions(A2b, D4, "a2_all")
         g2_all = load_row_to_all_partitions(g2, D4, "g2_all")
@@ -119,32 +118,32 @@ def tile_multiheadedattention_pa_kernel(tc, query, A1W, A1b, g1, b1, A2W, A2b, g
             )
 
         w1_grouped = {}
+        SHARES = [(512, 512), (512, 512), (512, 512), (512, 512)]
 
         def regroup_w1(g):
-            rows = w1_raw[g][:]
-            by_scalar = w_pool.tile([P, BANK, PACK], BF16, align_bytes=64)
-            regroup(nc.scalar.copy, by_scalar[:], rows[:, :, BANK : 2 * BANK])
-            by_vector = w_pool.tile([P, BANK, PACK], BF16, align_bytes=64)
-            regroup(nc.vector.tensor_copy, by_vector[:], rows[:, :, 0:BANK])
-            w1_grouped[g] = (by_vector, by_scalar)
+            first = 0
+            w1_grouped[g] = []
+            for copy, width, name in ((nc.vector.tensor_copy, SHARES[g][0], "v"), (nc.scalar.copy, SHARES[g][1], "s")):
+                while width:
+                    n = min(width, BANK)
+                    part = w_pool.tile([P, BANK, PACK], BF16, align_bytes=64, name="part_%s%d" % (name, first // 256), tag="part_" + name)
+                    regroup(copy, part[:, 0:n, :], w1_raw[g][:, :, first : first + n])
+                    w1_grouped[g].append((part, first, n))
+                    first += n
+                    width -= n
 
-        def quantise_w1(g, h):
-            cols = slice(h * BANK, (h + 1) * BANK)
+        def quantise_w1(g, k):
+            part, first, n = w1_grouped[g][k]
+            cols = slice(first, first + n)
             nc.vector.quantize_mx(
                 out=w1_codes[:, g, cols].bitcast(FP8X4),
                 scales=w1_scales[:, g, cols],
-                in_=w1_grouped[g][h][:].rearrange("p n t -> p (n t)"),
+                in_=part[:, 0:n, :].rearrange("p n t -> p (n t)"),
             )
-
-        def prepare_w1(g):
-            regroup_w1(g)
-            if g > 0:
-                quantise_w1(g - 1, 1)
-            quantise_w1(g, 0)
 
         def regroup_w2(c):
             grouped2 = keep.tile([P, D4, PACK], BF16, align_bytes=64, name="grouped2_%d" % c)
-            regroup(nc.scalar.copy, grouped2[:], w2_raw[c][:])
+            regroup(nc.vector.tensor_copy, grouped2[:], w2_raw[c][:])
             w2_grouped[c] = grouped2
 
         def quantise_w2(c):
@@ -176,22 +175,21 @@ def tile_multiheadedattention_pa_kernel(tc, query, A1W, A1b, g1, b1, A2W, A2b, g
             words = q_tiles[i][:].bitcast(F32)
             q_banks[i] = []
             for b in range(2):
-                qt = psum.tile([P, 2, 2, P], F32)
+                qt = psum.tile([P, 2, 2, P], F32, bufs=2)
                 for gg in range(2):
                     for u in range(2):
                         first = 256 * (2 * b + gg)
                         nc.tensor.transpose(qt[:, gg, u, :], words[:, first + u : first + 256 : 2], ident[:])
                 q_banks[i].append(qt)
 
-        def query_out_of_psum(i):
-            qg = work.tile([P, PASSES1 * P * PACK], BF16, align_bytes=64)
-            qg_words = qg[:].bitcast(F32).rearrange("p (g n u) -> p g n u", g=PASSES1, u=2)
-            for b in range(2):
-                nc.scalar.copy(
-                    out=qg_words[:, 2 * b : 2 * b + 2, :, :],
-                    in_=q_banks[i][b][:].rearrange("p g u n -> p g n u"),
-                )
-            q_grouped[i] = qg
+        def query_out_of_psum(i, b):
+            if b == 0:
+                qg = work.tile([P, PASSES1 * P * PACK], BF16, align_bytes=64)
+                q_grouped[i] = qg
+            qg_words = q_grouped[i][:].bitcast(F32).rearrange("p (g n u) -> p g n u", g=PASSES1, u=2)
+            nc.scalar.copy(
+                out=qg_words[:, 2 * b : 2 * b + 2, :, :], in_=q_banks[i][b][:].rearrange("p g u n -> p g n u"),
+            )
 
         def quantise_query(i):
             qc = work.tile([P, PASSES1 * P], U32, align_bytes=64, bufs=3)
@@ -200,21 +198,21 @@ def tile_multiheadedattention_pa_kernel(tc, query, A1W, A1b, g1, b1, A2W, A2b, g
             q_codes[i] = qc
             q_scales[i] = qs
 
-        def first_product(i, h):
+        def first_product_pass(i, h, g):
+            if g == 0:
+                acc1 = psum.tile([P, BANK], F32, bufs=3)
+                u_banks[i, h] = acc1
             cols = slice(h * BANK, (h + 1) * BANK)
-            acc1 = psum.tile([P, BANK], F32)
-            for g in range(PASSES1):
-                toks = slice(g * P, (g + 1) * P)
-                nc.tensor.matmul_mx(
-                    out=acc1[:],
-                    lhsT=q_codes[i][:, toks].bitcast(FP8X4),
-                    lhsT_scale=q_scales[i][:, toks],
-                    rhs=w1_codes[:, g, cols].bitcast(FP8X4),
-                    rhs_scale=w1_scales[:, g, cols],
-                    start=(g == 0),
-                    stop=(g == PASSES1 - 1),
-                )
-            u_banks[i, h] = acc1
+            toks = slice(g * P, (g + 1) * P)
+            nc.tensor.matmul_mx(
+                out=u_banks[i, h][:],
+                lhsT=q_codes[i][:, toks].bitcast(FP8X4),
+                lhsT_scale=q_scales[i][:, toks],
+                rhs=w1_codes[:, g, cols].bitcast(FP8X4),
+                rhs_scale=w1_scales[:, g, cols],
+                start=(g == 0),
+                stop=(g == PASSES1 - 1),
+            )
 
         def add_bias1(i):
             u = work.tile([P, D2], F32)
@@ -233,14 +231,14 @@ def tile_multiheadedattention_pa_kernel(tc, query, A1W, A1b, g1, b1, A2W, A2b, g
         def mean1(i):
             row_sum = stats1[i]["row_sum"]
             neg_mean = small.tile([P, 1], F32)
-            nc.vector.tensor_scalar(
-                out=neg_mean[:], in0=row_sum[:, 0:1], scalar1=row_sum[:, 1:2], scalar2=-1.0 / D2,
-                op0=ALU.add, op1=ALU.mult,
+            scaled = small.tile([P, HALVES1], F32)
+            nc.scalar.activation(
+                out=scaled[:], in_=row_sum[:], func=ACT.Identity, scale=-1.0 / D2, accum_out=neg_mean[:],
             )
             stats1[i]["neg_mean"] = neg_mean
 
         def deviation1(i):
-            squares = work.tile([P, D2], F32)
+            squares = work.tile([P, D2], F32, bufs=1)
             sq_sum = small.tile([P, 1], F32)
             nc.scalar.activation(
                 out=squares[:], in_=u_tiles[i][:], func=ACT.Square,
@@ -267,22 +265,22 @@ def tile_multiheadedattention_pa_kernel(tc, query, A1W, A1b, g1, b1, A2W, A2b, g
         def transpose_z(i):
             z_banks[i] = []
             for c in range(PASSES2):
-                zt = psum.tile([P, PACK, P], F32)
+                zt = psum.tile([P, PACK, P], F32, bufs=2)
                 for t in range(PACK):
                     first = K_PASS * c + P * t
                     nc.tensor.transpose(zt[:, t, :], z_tiles[i][:, first : first + P], ident[:])
                 z_banks[i].append(zt)
 
-        def gain_shift_relu1(i):
-            planes = work.tile([P, PACK, PASSES2, P], BF16)
-            for c in range(PASSES2):
-                for t in range(PACK):
-                    j = PACK * c + t
-                    nc.scalar.activation(
-                        out=planes[:, t, c, :], in_=z_banks[i][c][:, t, :], func=ACT.Relu,
-                        scale=gb[:, j : j + 1], bias=gb[:, D2 // P + j : D2 // P + j + 1],
-                    )
-            j_planes[i] = planes
+        def gain_shift_relu1(i, c):
+            if c == 0:
+                planes = work.tile([P, PACK, PASSES2, P], BF16)
+                j_planes[i] = planes
+            for t in range(PACK):
+                j = PACK * c + t
+                nc.scalar.activation(
+                    out=j_planes[i][:, t, c, :], in_=z_banks[i][c][:, t, :], func=ACT.Relu,
+                    scale=gb[:, j : j + 1], bias=gb[:, D2 // P + j : D2 // P + j + 1],
+                )
 
         def regroup_j1(i):
             jg = work.tile([P, PASSES2 * P, PACK], BF16, align_bytes=64)
@@ -300,7 +298,7 @@ def tile_multiheadedattention_pa_kernel(tc, query, A1W, A1b, g1, b1, A2W, A2b, g
             j_scales[i] = js
 
         def second_product(i):
-            acc2 = psum.tile([P, BANK], F32)
+            acc2 = psum.tile([P, BANK], F32, bufs=1)
             for c in range(PASSES2):
                 toks = slice(c * P, (c + 1) * P)
                 nc.tensor.matmul_mx(
@@ -315,7 +313,7 @@ def tile_multiheadedattention_pa_kernel(tc, query, A1W, A1b, g1, b1, A2W, A2b, g
             w_banks[i] = acc2
 
         def add_bias2(i):
-            w = work.tile([P, D4], F32, bufs=3)
+            w = work.tile([P, D4], F32, bufs=4)
             row_sum2 = small.tile([P, 1], F32)
             nc.vector.scalar_tensor_tensor(
                 out=w[:], in0=w_banks[i][:], scalar=1.0, in1=a2_all[:],
@@ -326,14 +324,13 @@ def tile_multiheadedattention_pa_kernel(tc, query, A1W, A1b, g1, b1, A2W, A2b, g
 
         def mean2(i):
             neg_mean2 = small.tile([P, 1], F32)
-            nc.vector.tensor_scalar(
-                out=neg_mean2[:], in0=stats2[i]["row_sum"][:], scalar1=-1.0 / D4, scalar2=None,
-                op0=ALU.mult,
+            nc.scalar.activation(
+                out=neg_mean2[:], in_=stats2[i]["row_sum"][:], func=ACT.Identity, scale=-1.0 / D4,
             )
             stats2[i]["neg_mean"] = neg_mean2
 
         def deviation2(i):
-            squares2 = work.tile([P, D4], F32)
+            squares2 = work.tile([P, D4], F32, bufs=1)
             sq_sum2 = small.tile([P, 1], F32)
             nc.scalar.activation(
                 out=squares2[:], in_=w_tiles[i][:], func=ACT.Square,
@@ -352,7 +349,7 @@ def tile_multiheadedattention_pa_kernel(tc, query, A1W, A1b, g1, b1, A2W, A2b, g
         x_tiles = {}
 
         def centre_gain2(i):
-            x = work.tile([P, D4], F32)
+            x = work.tile([P, D4], F32, bufs=4)
             nc.vector.scalar_tensor_tensor(
                 out=x[:], in0=w_tiles[i][:], scalar=stats2[i]["neg_mean"][:], in1=g2_all[:],
                 op0=ALU.add, op1=ALU.mult,
@@ -360,7 +357,7 @@ def tile_multiheadedattention_pa_kernel(tc, query, A1W, A1b, g1, b1, A2W, A2b, g
             x_tiles[i] = x
 
         def scale_shift2(i):
-            y = work.tile([P, D4], F32)
+            y = work.tile([P, D4], F32, bufs=4)
             nc.vector.scalar_tensor_tensor(
                 out=y[:], in0=x_tiles[i][:], scalar=stats2[i]["rstd"][:], in1=b2_all[:],
                 op0=ALU.mult, op1=ALU.add,
@@ -369,57 +366,87 @@ def tile_multiheadedattention_pa_kernel(tc, query, A1W, A1b, g1, b1, A2W, A2b, g
 
         def relu_and_store(i):
             result = work.tile([P, D4], F32, bufs=3)
-            nc.scalar.activation(out=result[:], in_=y_tiles[i][:], func=ACT.Relu)
+            if False:
+                nc.vector.tensor_scalar(
+                    out=result[:], in0=y_tiles[i][:], scalar1=0.0, scalar2=None, op0=ALU.max,
+                )
+            else:
+                nc.scalar.activation(out=result[:], in_=y_tiles[i][:], func=ACT.Relu)
             nc.sync.dma_start(out=out_rows[i * P : (i + 1) * P, :], in_=result[:])
+
+        last = PASSES1 - 1
+
+        def bring_query(i):
+            transpose_query(i)
+            for b in range(2):
+                query_out_of_psum(i, b)
+
+        bring_query(0)
+        for g in range(PASSES1):
+            regroup_w1(g)
+            if g == 0:
+                quantise_query(0)
+            else:
+                for h in range(HALVES1):
+                    quantise_w1(g - 1, h)
+                    first_product_pass(0, h, g - 1)
+        bring_query(1)
+        nc.vector.tensor_copy(
+            out=a1_perm[:], in_=a1_all[:].rearrange("p (c m t) -> p c t m", c=HALVES1, t=PACK),
+        )
+        for h in range(HALVES1):
+            quantise_w1(last, h)
+            first_product_pass(0, h, last)
+        nc.vector.tensor_copy(out=gb[:, 0 : D2 // P], in_=g1_raw[:].rearrange("p c t -> p (c t)"))
+        nc.vector.tensor_copy(out=gb[:, D2 // P : 2 * D2 // P], in_=b1_raw[:].rearrange("p c t -> p (c t)"))
+        quantise_query(1)
+        bring_query(2)
+        for i in range(Q_BUFS, Q_BUFS + 2):
+            load_query(i)
 
         def run(step, i, *more):
             if 0 <= i < TILES:
                 step(i, *more)
 
+        def new_query(i, step, *more):
+            if i >= HEAD[step]:
+                run(step, i, *more)
+
+        HEAD = {quantise_query: 2, transpose_query: 3, query_out_of_psum: 3}
+
         def period(i):
-            if Q_BUFS <= i + 1 + Q_BUFS < TILES:
-                load_query(i + 1 + Q_BUFS)
-            run(first_product, i, 0)
-            run(transpose_query, i + 2)
-            run(first_product, i, 1)
-            run(transpose_z, i - 2)
-            run(regroup_j1, i - 3)
-            run(mean2, i - 4)
-            run(quantise_query, i + 1)
-            if i == W1_PERIOD:
-                for g in range(PASSES1):
-                    prepare_w1(g)
-                quantise_w1(PASSES1 - 1, 1)
-                nc.vector.tensor_copy(
-                    out=gb[:, 0 : D2 // P], in_=g1_raw[:].rearrange("p c t -> p (c t)")
-                )
-                nc.vector.tensor_copy(
-                    out=gb[:, D2 // P : 2 * D2 // P], in_=b1_raw[:].rearrange("p c t -> p (c t)")
-                )
-                nc.vector.tensor_copy(
-                    out=a1_perm[:], in_=a1_all[:].rearrange("p (c m t) -> p c t m", c=HALVES1, t=PACK),
-                )
-            run(quantise_j1, i - 3)
-            run(centre_gain2, i - 4)
-            run(second_product, i - 3)
-            run(deviation1, i - 1)
-            run(deviation2, i - 4)
-            run(query_out_of_psum, i + 2)
-            if i == W2_REGROUP_PERIOD:
-                for c in range(PASSES2):
-                    regroup_w2(c)
-            run(inverse_deviation1, i - 1)
-            run(inverse_deviation2, i - 4)
-            run(gain_shift_relu1, i - 2)
-            run(relu_and_store, i - 5)
+            run(load_query, i + 2 + Q_BUFS)
             run(add_bias1, i)
-            run(normalise1, i - 1)
-            run(scale_shift2, i - 4)
+            run(quantise_j1, i - 3)
+            run(second_product, i - 3)
+            for g in range(PASSES1):
+                run(first_product_pass, i + 1, 0, g)
+            for g in range(PASSES1):
+                run(first_product_pass, i + 1, 1, g)
             run(mean1, i)
-            run(add_bias2, i - 3)
-            if i == W2_QUANTISE_PERIOD:
+            run(deviation2, i - 5)
+            run(deviation1, i)
+            run(mean2, i - 4)
+            run(inverse_deviation1, i)
+            run(scale_shift2, i - 6)
+            if i < PASSES2:
+                regroup_w2(i)
+            run(normalise1, i - 1)
+            run(transpose_z, i - 1)
+            new_query(i + 3, transpose_query)
+            run(centre_gain2, i - 5)
+            if i == 2:
                 for c in range(PASSES2):
                     quantise_w2(c)
+            run(regroup_j1, i - 2)
+            run(add_bias2, i - 3)
+            new_query(i + 2, quantise_query)
+            for c in range(2):
+                run(gain_shift_relu1, i - 1, c)
+            run(inverse_deviation2, i - 5)
+            for b in range(2):
+                new_query(i + 3, query_out_of_psum, b)
+            run(relu_and_store, i - 6)
 
-        for i in range(-2, TILES + 5):
+        for i in range(TILES + 7):
             period(i)

@@ -214,19 +214,23 @@ def tile_multiheadedattention_pa_kernel(tc, query, A1W, A1b, g1, b1, A2W, A2b, g
                 stop=(g == PASSES1 - 1),
             )
 
-        def add_bias1(i):
-            u = work.tile([P, D2], F32)
-            row_sum = small.tile([P, HALVES1], F32)
-            for h in range(HALVES1):
-                cols = slice(h * BANK, (h + 1) * BANK)
-                nc.vector.scalar_tensor_tensor(
-                    out=u[:, cols].rearrange("p (t m) -> p t m", t=PACK),
-                    in0=u_banks[i, h][:].rearrange("p (m t) -> p t m", t=PACK),
-                    scalar=1.0, in1=a1_perm[:, h, :, :],
-                    op0=ALU.mult, op1=ALU.add, accum_out=row_sum[:, h : h + 1],
-                )
-            u_tiles[i] = u
-            stats1[i] = {"row_sum": row_sum}
+        def first_product(i, h):
+            for g in range(PASSES1):
+                first_product_pass(i, h, g)
+
+        def add_bias1(i, h):
+            if i not in u_tiles:
+                u = work.tile([P, D2], F32)
+                u_tiles[i] = u
+                row_sum = small.tile([P, HALVES1], F32)
+                stats1[i] = {"row_sum": row_sum}
+            cols = slice(h * BANK, (h + 1) * BANK)
+            nc.vector.scalar_tensor_tensor(
+                out=u_tiles[i][:, cols].rearrange("p (t m) -> p t m", t=PACK),
+                in0=u_banks[i, h][:].rearrange("p (m t) -> p t m", t=PACK),
+                scalar=1.0, in1=a1_perm[:, h, :, :],
+                op0=ALU.mult, op1=ALU.add, accum_out=stats1[i]["row_sum"][:, h : h + 1],
+            )
 
         def mean1(i):
             row_sum = stats1[i]["row_sum"]
@@ -262,23 +266,21 @@ def tile_multiheadedattention_pa_kernel(tc, query, A1W, A1b, g1, b1, A2W, A2b, g
             )
             z_tiles[i] = z
 
-        def transpose_z(i):
-            z_banks[i] = []
-            for c in range(PASSES2):
-                zt = psum.tile([P, PACK, P], F32, bufs=2)
-                for t in range(PACK):
-                    first = K_PASS * c + P * t
-                    nc.tensor.transpose(zt[:, t, :], z_tiles[i][:, first : first + P], ident[:])
-                z_banks[i].append(zt)
+        def transpose_z(i, c):
+            zt = psum.tile([P, PACK, P], F32, bufs=2)
+            for t in range(PACK):
+                first = K_PASS * c + P * t
+                nc.tensor.transpose(zt[:, t, :], z_tiles[i][:, first : first + P], ident[:])
+            z_banks[i, c] = zt
 
         def gain_shift_relu1(i, c):
-            if c == 0:
+            if i not in j_planes:
                 planes = work.tile([P, PACK, PASSES2, P], BF16)
                 j_planes[i] = planes
             for t in range(PACK):
                 j = PACK * c + t
                 nc.scalar.activation(
-                    out=j_planes[i][:, t, c, :], in_=z_banks[i][c][:, t, :], func=ACT.Relu,
+                    out=j_planes[i][:, t, c, :], in_=z_banks[i, c][:, t, :], func=ACT.Relu,
                     scale=gb[:, j : j + 1], bias=gb[:, D2 // P + j : D2 // P + j + 1],
                 )
 
@@ -391,16 +393,16 @@ def tile_multiheadedattention_pa_kernel(tc, query, A1W, A1b, g1, b1, A2W, A2b, g
                     quantise_w1(g - 1, h)
                     first_product_pass(0, h, g - 1)
         bring_query(1)
-        nc.vector.tensor_copy(
-            out=a1_perm[:], in_=a1_all[:].rearrange("p (c m t) -> p c t m", c=HALVES1, t=PACK),
-        )
         for h in range(HALVES1):
             quantise_w1(last, h)
             first_product_pass(0, h, last)
+        nc.vector.tensor_copy(
+            out=a1_perm[:], in_=a1_all[:].rearrange("p (c m t) -> p c t m", c=HALVES1, t=PACK),
+        )
         nc.vector.tensor_copy(out=gb[:, 0 : D2 // P], in_=g1_raw[:].rearrange("p c t -> p (c t)"))
         nc.vector.tensor_copy(out=gb[:, D2 // P : 2 * D2 // P], in_=b1_raw[:].rearrange("p c t -> p (c t)"))
         quantise_query(1)
-        bring_query(2)
+        regroup_w2(0)
         for i in range(Q_BUFS, Q_BUFS + 2):
             load_query(i)
 
@@ -412,41 +414,42 @@ def tile_multiheadedattention_pa_kernel(tc, query, A1W, A1b, g1, b1, A2W, A2b, g
             if i >= HEAD[step]:
                 run(step, i, *more)
 
-        HEAD = {quantise_query: 2, transpose_query: 3, query_out_of_psum: 3}
+        HEAD = {quantise_query: 2, transpose_query: 2, query_out_of_psum: 2}
 
         def period(i):
             run(load_query, i + 2 + Q_BUFS)
-            run(add_bias1, i)
-            run(quantise_j1, i - 3)
-            run(second_product, i - 3)
-            for g in range(PASSES1):
-                run(first_product_pass, i + 1, 0, g)
-            for g in range(PASSES1):
-                run(first_product_pass, i + 1, 1, g)
-            run(mean1, i)
-            run(deviation2, i - 5)
-            run(deviation1, i)
-            run(mean2, i - 4)
-            run(inverse_deviation1, i)
-            run(scale_shift2, i - 6)
-            if i < PASSES2:
-                regroup_w2(i)
-            run(normalise1, i - 1)
-            run(transpose_z, i - 1)
-            new_query(i + 3, transpose_query)
+            run(add_bias1, i, 1)
+            if i > 0:
+                run(first_product, i, 0)
+            run(gain_shift_relu1, i - 3, 1)
+            run(mean1, i - 1)
+            run(inverse_deviation2, i - 5)
+            run(gain_shift_relu1, i - 3, 0)
             run(centre_gain2, i - 5)
-            if i == 2:
+            run(add_bias2, i - 4)
+            run(regroup_j1, i - 3)
+            if i == 1:
+                regroup_w2(1)
+            run(add_bias1, i, 0)
+            run(quantise_j1, i - 3)
+            new_query(i + 2, transpose_query)
+            run(transpose_z, i - 2, 1)
+            run(first_product, i + 1, 1)
+            run(transpose_z, i - 2, 0)
+            run(second_product, i - 3)
+            run(deviation1, i - 1)
+            run(relu_and_store, i - 7)
+            run(mean2, i - 4)
+            run(inverse_deviation1, i - 1)
+            for b in range(2):
+                new_query(i + 2, query_out_of_psum, b)
+            run(deviation2, i - 4)
+            run(scale_shift2, i - 5)
+            run(normalise1, i - 1)
+            if i == 1:
                 for c in range(PASSES2):
                     quantise_w2(c)
-            run(regroup_j1, i - 2)
-            run(add_bias2, i - 3)
             new_query(i + 2, quantise_query)
-            for c in range(2):
-                run(gain_shift_relu1, i - 1, c)
-            run(inverse_deviation2, i - 5)
-            for b in range(2):
-                new_query(i + 3, query_out_of_psum, b)
-            run(relu_and_store, i - 6)
 
-        for i in range(TILES + 7):
+        for i in range(TILES + 8):
             period(i)

@@ -368,7 +368,7 @@ def tile_multiheadedattention_pa_kernel(tc, query, A1W, A1b, g1, b1, A2W, A2b, g
 
         def relu_and_store(i):
             result = work.tile([P, D4], F32, bufs=3)
-            if False:
+            if i % 2:
                 nc.vector.tensor_scalar(
                     out=result[:], in0=y_tiles[i][:], scalar1=0.0, scalar2=None, op0=ALU.max,
                 )
@@ -378,31 +378,30 @@ def tile_multiheadedattention_pa_kernel(tc, query, A1W, A1b, g1, b1, A2W, A2b, g
 
         last = PASSES1 - 1
 
-        def bring_query(i):
-            transpose_query(i)
-            for b in range(2):
-                query_out_of_psum(i, b)
-
-        bring_query(0)
+        transpose_query(0)
+        for b in range(2):
+            query_out_of_psum(0, b)
         for g in range(PASSES1):
             regroup_w1(g)
             if g == 0:
                 quantise_query(0)
-            else:
+            if g == last:
+                transpose_query(1)
+                for b in range(2):
+                    query_out_of_psum(1, b)
+            if g > 0:
                 for h in range(HALVES1):
                     quantise_w1(g - 1, h)
                     first_product_pass(0, h, g - 1)
-        bring_query(1)
         for h in range(HALVES1):
             quantise_w1(last, h)
             first_product_pass(0, h, last)
+        quantise_query(1)
         nc.vector.tensor_copy(
             out=a1_perm[:], in_=a1_all[:].rearrange("p (c m t) -> p c t m", c=HALVES1, t=PACK),
         )
-        nc.vector.tensor_copy(out=gb[:, 0 : D2 // P], in_=g1_raw[:].rearrange("p c t -> p (c t)"))
-        nc.vector.tensor_copy(out=gb[:, D2 // P : 2 * D2 // P], in_=b1_raw[:].rearrange("p c t -> p (c t)"))
-        quantise_query(1)
-        regroup_w2(0)
+        for h in range(HALVES1):
+            add_bias1(0, h)
         for i in range(Q_BUFS, Q_BUFS + 2):
             load_query(i)
 
@@ -418,7 +417,8 @@ def tile_multiheadedattention_pa_kernel(tc, query, A1W, A1b, g1, b1, A2W, A2b, g
 
         def period(i):
             run(load_query, i + 2 + Q_BUFS)
-            run(add_bias1, i, 1)
+            if i > 0:
+                run(add_bias1, i, 1)
             if i > 0:
                 run(first_product, i, 0)
             run(gain_shift_relu1, i - 3, 1)
@@ -428,17 +428,16 @@ def tile_multiheadedattention_pa_kernel(tc, query, A1W, A1b, g1, b1, A2W, A2b, g
             run(centre_gain2, i - 5)
             run(add_bias2, i - 4)
             run(regroup_j1, i - 3)
-            if i == 1:
-                regroup_w2(1)
-            run(add_bias1, i, 0)
+            if i > 0:
+                run(add_bias1, i, 0)
             run(quantise_j1, i - 3)
             new_query(i + 2, transpose_query)
-            run(transpose_z, i - 2, 1)
             run(first_product, i + 1, 1)
+            run(transpose_z, i - 2, 1)
             run(transpose_z, i - 2, 0)
             run(second_product, i - 3)
             run(deviation1, i - 1)
-            run(relu_and_store, i - 7)
+            run(relu_and_store, i - 6)
             run(mean2, i - 4)
             run(inverse_deviation1, i - 1)
             for b in range(2):
@@ -446,10 +445,16 @@ def tile_multiheadedattention_pa_kernel(tc, query, A1W, A1b, g1, b1, A2W, A2b, g
             run(deviation2, i - 4)
             run(scale_shift2, i - 5)
             run(normalise1, i - 1)
+            new_query(i + 2, quantise_query)
+            if i == 0:
+                regroup_w2(0)
+                nc.vector.tensor_copy(out=gb[:, 0 : D2 // P], in_=g1_raw[:].rearrange("p c t -> p (c t)"))
+                nc.vector.tensor_copy(out=gb[:, D2 // P : 2 * D2 // P], in_=b1_raw[:].rearrange("p c t -> p (c t)"))
             if i == 1:
+                regroup_w2(1)
+            if i == 2:
                 for c in range(PASSES2):
                     quantise_w2(c)
-            new_query(i + 2, quantise_query)
 
         for i in range(TILES + 8):
             period(i)

@@ -55,6 +55,10 @@ def tile_multiheadedattention_pa_kernel(tc, query, A1W, A1b, g1, b1, A2W, A2b, g
         nc.vector.memset(eps[:], EPS)
         table_warm = keep.tile([P, 1], F32)
         nc.scalar.activation(out=table_warm[:], in_=eps[:], func=ACT.Abs_reciprocal_sqrt)
+        ones = keep.tile([P, P], BF16)
+        nc.gpsimd.memset(ones[:], 1.0)
+        a1_row = keep.tile([P, D2], BF16)
+        nc.vector.memset(a1_row[:], 0.0)
 
 
         q_tiles = {}
@@ -82,25 +86,27 @@ def tile_multiheadedattention_pa_kernel(tc, query, A1W, A1b, g1, b1, A2W, A2b, g
             return spread
 
         load_query(0)
+        nc.scalar.dma_start(out=a1_row[0:1, :], in_=A1b.rearrange("(o n) -> o n", o=1))
         load_w1(0)
         load_w1(1)
-        a1_all = load_row_to_all_partitions(A1b, D2, "a1_all")
         load_w1(2)
         load_w1(3)
         load_query(1)
+        load_query(2)
+        for c in range(PASSES2):
+            load_w2(c)
         g1_raw = keep.tile([P, PASSES2, PACK], BF16)
         nc.sync.dma_start(out=g1_raw[:], in_=g1_view)
         b1_raw = keep.tile([P, PASSES2, PACK], BF16)
         nc.sync.dma_start(out=b1_raw[:], in_=b1_view)
-        load_query(2)
-        for c in range(PASSES2):
-            load_w2(c)
         load_query(3)
+        load_query(4)
         a2_all = load_row_to_all_partitions(A2b, D4, "a2_all")
+        load_query(5)
         g2_all = load_row_to_all_partitions(g2, D4, "g2_all")
+        load_query(6)
         b2_all = load_row_to_all_partitions(b2, D4, "b2_all")
-        for i in range(4, Q_BUFS):
-            load_query(i)
+        load_query(7)
 
         gb = keep.tile([P, 2 * D2 // P], F32)
         a1_perm = keep.tile([P, HALVES1, PACK, P], BF16)
@@ -381,6 +387,13 @@ def tile_multiheadedattention_pa_kernel(tc, query, A1W, A1b, g1, b1, A2W, A2b, g
         transpose_query(0)
         for b in range(2):
             query_out_of_psum(0, b)
+        a1_banks = []
+        for h in range(HALVES1):
+            a1_bank = psum.tile([P, BANK], F32, tag="zt", bufs=2)
+            nc.tensor.matmul(
+                a1_bank[:], lhsT=ones[:], rhs=a1_row[:, h * BANK : (h + 1) * BANK], start=True, stop=True,
+            )
+            a1_banks.append(a1_bank)
         for g in range(PASSES1):
             regroup_w1(g)
             if g == 0:
@@ -397,9 +410,10 @@ def tile_multiheadedattention_pa_kernel(tc, query, A1W, A1b, g1, b1, A2W, A2b, g
             quantise_w1(last, h)
             first_product_pass(0, h, last)
         quantise_query(1)
-        nc.vector.tensor_copy(
-            out=a1_perm[:], in_=a1_all[:].rearrange("p (c m t) -> p c t m", c=HALVES1, t=PACK),
-        )
+        for h in range(HALVES1):
+            nc.vector.tensor_copy(
+                out=a1_perm[:, h, :, :], in_=a1_banks[h][:].rearrange("p (m t) -> p t m", t=PACK),
+            )
         for h in range(HALVES1):
             add_bias1(0, h)
         for i in range(Q_BUFS, Q_BUFS + 2):

@@ -49,16 +49,16 @@ def tile_multiheadedattention_pa_kernel(tc, query, A1W, A1b, g1, b1, A2W, A2b, g
         psum = ctx.enter_context(tc.psum_pool(name="psum", bufs=4))
         ctx.enter_context(tc.manual_schedule())
 
+        a1_raw = keep.tile([P, PASSES2, PACK], BF16)
+        nc.sync.dma_start(out=a1_raw[:], in_=A1b.rearrange("(c p t) -> p c t", c=PASSES2, p=P, t=PACK))
         ident = keep.tile([P, P], F32)
         make_identity(nc, ident[:])
+        ident_bf16 = keep.tile([P, P], BF16)
+        nc.gpsimd.tensor_copy(out=ident_bf16[:], in_=ident[:])
         eps = keep.tile([P, 1], F32)
         nc.vector.memset(eps[:], EPS)
         table_warm = keep.tile([P, 1], F32)
         nc.scalar.activation(out=table_warm[:], in_=eps[:], func=ACT.Abs_reciprocal_sqrt)
-        ones = keep.tile([P, P], BF16)
-        nc.gpsimd.memset(ones[:], 1.0)
-        a1_row = keep.tile([P, D2], BF16)
-        nc.vector.memset(a1_row[:], 0.0)
 
 
         q_tiles = {}
@@ -86,7 +86,6 @@ def tile_multiheadedattention_pa_kernel(tc, query, A1W, A1b, g1, b1, A2W, A2b, g
             return spread
 
         load_query(0)
-        nc.scalar.dma_start(out=a1_row[0:1, :], in_=A1b.rearrange("(o n) -> o n", o=1))
         load_w1(0)
         load_w1(1)
         load_w1(2)
@@ -374,7 +373,7 @@ def tile_multiheadedattention_pa_kernel(tc, query, A1W, A1b, g1, b1, A2W, A2b, g
 
         def relu_and_store(i):
             result = work.tile([P, D4], F32, bufs=3)
-            if i % 2:
+            if i == TILES - 1:
                 nc.vector.tensor_scalar(
                     out=result[:], in0=y_tiles[i][:], scalar1=0.0, scalar2=None, op0=ALU.max,
                 )
@@ -384,16 +383,17 @@ def tile_multiheadedattention_pa_kernel(tc, query, A1W, A1b, g1, b1, A2W, A2b, g
 
         last = PASSES1 - 1
 
+        for h in range(HALVES1):
+            a1_bank = psum.tile([P, PACK, P], F32, tag="zt", bufs=2)
+            for t in range(PACK):
+                nc.tensor.matmul(
+                    a1_bank[:, t, :], lhsT=a1_raw[:, h, t : t + 1].to_broadcast([P, P]), rhs=ident_bf16[:],
+                    start=True, stop=True,
+                )
+            nc.vector.tensor_copy(out=a1_perm[:, h, :, :], in_=a1_bank[:])
         transpose_query(0)
         for b in range(2):
             query_out_of_psum(0, b)
-        a1_banks = []
-        for h in range(HALVES1):
-            a1_bank = psum.tile([P, BANK], F32, tag="zt", bufs=2)
-            nc.tensor.matmul(
-                a1_bank[:], lhsT=ones[:], rhs=a1_row[:, h * BANK : (h + 1) * BANK], start=True, stop=True,
-            )
-            a1_banks.append(a1_bank)
         for g in range(PASSES1):
             regroup_w1(g)
             if g == 0:
@@ -410,10 +410,6 @@ def tile_multiheadedattention_pa_kernel(tc, query, A1W, A1b, g1, b1, A2W, A2b, g
             quantise_w1(last, h)
             first_product_pass(0, h, last)
         quantise_query(1)
-        for h in range(HALVES1):
-            nc.vector.tensor_copy(
-                out=a1_perm[:, h, :, :], in_=a1_banks[h][:].rearrange("p (m t) -> p t m", t=PACK),
-            )
         for h in range(HALVES1):
             add_bias1(0, h)
         for i in range(Q_BUFS, Q_BUFS + 2):

from contextlib import ExitStack

import concourse.mybir as mybir
from concourse.masks import make_identity

F32 = mybir.dt.float32
BF16 = mybir.dt.bfloat16
U32 = mybir.dt.uint32
U8 = mybir.dt.uint8
FP8X4 = mybir.dt.float8_e4m3fn_x4
ALU = mybir.AluOpType
ACT = mybir.ActivationFunctionType

P = 128
PACK = 4
K_PASS = P * PACK
BANK = 512

TOKENS = 128 * 17
D = 2048
D2 = 1024
D4 = 512
EPS = 1e-5
TILES = TOKENS // P
PASSES1 = D // K_PASS
PASSES2 = D2 // K_PASS
HALVES1 = D2 // BANK

FLOPS = 2 * TOKENS * (D * D2 + D2 * D4)

Q_BUFS = 8


def tile_multiheadedattention_pa_kernel(tc, query, A1W, A1b, g1, b1, A2W, A2b, g2, b2, out):
    nc = tc.nc
    q_rows = query.flatten_outer_dims()
    out_rows = out.flatten_outer_dims()
    w1_view = A1W.rearrange("(g p t) n -> g p t n", g=PASSES1, p=P, t=PACK)
    w2_view = A2W.rearrange("(c p t) n -> c p t n", c=PASSES2, p=P, t=PACK)
    g1_view = g1.rearrange("(c p t) -> p c t", c=PASSES2, p=P, t=PACK)
    b1_view = b1.rearrange("(c p t) -> p c t", c=PASSES2, p=P, t=PACK)

    with ExitStack() as ctx:
        keep = ctx.enter_context(tc.tile_pool(name="keep", bufs=1))
        q_pool = ctx.enter_context(tc.tile_pool(name="q_pool", bufs=Q_BUFS))
        w_pool = ctx.enter_context(tc.tile_pool(name="w_pool", bufs=2))
        work = ctx.enter_context(tc.tile_pool(name="work", bufs=2))
        small = ctx.enter_context(tc.tile_pool(name="small", bufs=8))
        psum = ctx.enter_context(tc.psum_pool(name="psum", bufs=4))
        ctx.enter_context(tc.manual_schedule())

        a1_raw = keep.tile([P, PASSES2, PACK], BF16)
        nc.sync.dma_start(out=a1_raw[:], in_=A1b.rearrange("(c p t) -> p c t", c=PASSES2, p=P, t=PACK))
        ident = keep.tile([P, P], F32)
        make_identity(nc, ident[:])
        ident_bf16 = keep.tile([P, P], BF16)
        nc.gpsimd.tensor_copy(out=ident_bf16[:], in_=ident[:])
        eps = keep.tile([P, 1], F32)
        nc.vector.memset(eps[:], EPS)
        table_warm = keep.tile([P, 1], F32)
        nc.scalar.activation(out=table_warm[:], in_=eps[:], func=ACT.Abs_reciprocal_sqrt)


        q_tiles = {}
        w1_raw = {}
        w2_raw = {}

        def load_query(i):
            q_sb = q_pool.tile([P, D], BF16)
            nc.sync.dma_start(out=q_sb[:], in_=q_rows[i * P : (i + 1) * P, :])
            q_tiles[i] = q_sb

        def load_w1(g):
            raw1 = keep.tile([P, PACK, D2], BF16, name="raw1_%d" % g)
            nc.sync.dma_start(out=raw1[:], in_=w1_view[g])
            w1_raw[g] = raw1

        def load_w2(c):
            raw2 = keep.tile([P, PACK, D4], BF16, name="raw2_%d" % c)
            nc.sync.dma_start(out=raw2[:], in_=w2_view[c])
            w2_raw[c] = raw2

        def load_row_to_all_partitions(vec, width, name):
            spread = keep.tile([P, width], BF16, name=name)
            nc.sync.dma_start(out=spread[:], in_=vec.partition_broadcast(P))
            return spread

        load_query(0)
        load_w1(0)
        load_w1(1)
        load_w1(2)
        load_w1(3)
        load_query(1)
        load_query(2)
        for c in range(PASSES2):
            load_w2(c)
        g1_raw = keep.tile([P, PASSES2, PACK], BF16)
        nc.sync.dma_start(out=g1_raw[:], in_=g1_view)
        b1_raw = keep.tile([P, PASSES2, PACK], BF16)
        nc.sync.dma_start(out=b1_raw[:], in_=b1_view)
        load_query(3)
        load_query(4)
        a2_all = load_row_to_all_partitions(A2b, D4, "a2_all")
        load_query(5)
        g2_all = load_row_to_all_partitions(g2, D4, "g2_all")
        load_query(6)
        b2_all = load_row_to_all_partitions(b2, D4, "b2_all")
        load_query(7)

        gb = keep.tile([P, 2 * D2 // P], F32)
        a1_perm = keep.tile([P, HALVES1, PACK, P], BF16)

        w1_codes = keep.tile([P, PASSES1, D2], U32, align_bytes=64)
        w1_scales = keep.tile([P, PASSES1, D2], U8, align_bytes=64)
        w2_codes = keep.tile([P, PASSES2, D4], U32, align_bytes=64)
        w2_scales = keep.tile([P, PASSES2, D4], U8, align_bytes=64)
        w2_grouped = {}

        def regroup(copy, dst, src):
            copy(
                out=dst.rearrange("p (c i) t -> p c t i", i=4),
                in_=src.rearrange("p t (c i) -> p c t i", i=4),
            )

        w1_grouped = {}
        SHARES = [(512, 512), (512, 512), (512, 512), (512, 512)]

        def regroup_w1(g):
            first = 0
            w1_grouped[g] = []
            for copy, width, name in ((nc.vector.tensor_copy, SHARES[g][0], "v"), (nc.scalar.copy, SHARES[g][1], "s")):
                while width:
                    n = min(width, BANK)
                    part = w_pool.tile([P, BANK, PACK], BF16, align_bytes=64, name="part_%s%d" % (name, first // 256), tag="part_" + name)
                    regroup(copy, part[:, 0:n, :], w1_raw[g][:, :, first : first + n])
                    w1_grouped[g].append((part, first, n))
                    first += n
                    width -= n

        def quantise_w1(g, k):
            part, first, n = w1_grouped[g][k]
            cols = slice(first, first + n)
            nc.vector.quantize_mx(
                out=w1_codes[:, g, cols].bitcast(FP8X4),
                scales=w1_scales[:, g, cols],
                in_=part[:, 0:n, :].rearrange("p n t -> p (n t)"),
            )

        def regroup_w2(c):
            grouped2 = keep.tile([P, D4, PACK], BF16, align_bytes=64, name="grouped2_%d" % c)
            regroup(nc.vector.tensor_copy, grouped2[:], w2_raw[c][:])
            w2_grouped[c] = grouped2

        def quantise_w2(c):
            nc.vector.quantize_mx(
                out=w2_codes[:, c, :].bitcast(FP8X4),
                scales=w2_scales[:, c, :],
                in_=w2_grouped[c][:].rearrange("p n t -> p (n t)"),
            )

        q_banks = {}
        q_grouped = {}
        q_codes = {}
        q_scales = {}
        u_banks = {}
        u_tiles = {}
        stats1 = {}
        z_tiles = {}
        z_banks = {}
        j_planes = {}
        j_grouped = {}
        j_codes = {}
        j_scales = {}
        w_banks = {}
        w_tiles = {}
        stats2 = {}
        y_tiles = {}

        def transpose_query(i):
            words = q_tiles[i][:].bitcast(F32)
            q_banks[i] = []
            for b in range(2):
                qt = psum.tile([P, 2, 2, P], F32, bufs=2)
                for gg in range(2):
                    for u in range(2):
                        first = 256 * (2 * b + gg)
                        nc.tensor.transpose(qt[:, gg, u, :], words[:, first + u : first + 256 : 2], ident[:])
                q_banks[i].append(qt)

        def query_out_of_psum(i, b):
            if b == 0:
                qg = work.tile([P, PASSES1 * P * PACK], BF16, align_bytes=64)
                q_grouped[i] = qg
            qg_words = q_grouped[i][:].bitcast(F32).rearrange("p (g n u) -> p g n u", g=PASSES1, u=2)
            nc.scalar.copy(
                out=qg_words[:, 2 * b : 2 * b + 2, :, :], in_=q_banks[i][b][:].rearrange("p g u n -> p g n u"),
            )

        def quantise_query(i):
            qc = work.tile([P, PASSES1 * P], U32, align_bytes=64, bufs=3)
            qs = work.tile([P, PASSES1 * P], U8, align_bytes=64, bufs=3)
            nc.vector.quantize_mx(out=qc[:].bitcast(FP8X4), scales=qs[:], in_=q_grouped[i][:])
            q_codes[i] = qc
            q_scales[i] = qs

        def first_product_pass(i, h, g):
            if g == 0:
                acc1 = psum.tile([P, BANK], F32, bufs=3)
                u_banks[i, h] = acc1
            cols = slice(h * BANK, (h + 1) * BANK)
            toks = slice(g * P, (g + 1) * P)
            nc.tensor.matmul_mx(
                out=u_banks[i, h][:],
                lhsT=q_codes[i][:, toks].bitcast(FP8X4),
                lhsT_scale=q_scales[i][:, toks],
                rhs=w1_codes[:, g, cols].bitcast(FP8X4),
                rhs_scale=w1_scales[:, g, cols],
                start=(g == 0),
                stop=(g == PASSES1 - 1),
            )

        def first_product(i, h):
            for g in range(PASSES1):
                first_product_pass(i, h, g)

        def add_bias1(i, h):
            if i not in u_tiles:
                u = work.tile([P, D2], F32)
                u_tiles[i] = u
                row_sum = small.tile([P, HALVES1], F32)
                stats1[i] = {"row_sum": row_sum}
            cols = slice(h * BANK, (h + 1) * BANK)
            nc.vector.scalar_tensor_tensor(
                out=u_tiles[i][:, cols].rearrange("p (t m) -> p t m", t=PACK),
                in0=u_banks[i, h][:].rearrange("p (m t) -> p t m", t=PACK),
                scalar=1.0, in1=a1_perm[:, h, :, :],
                op0=ALU.mult, op1=ALU.add, accum_out=stats1[i]["row_sum"][:, h : h + 1],
            )

        def mean1(i):
            row_sum = stats1[i]["row_sum"]
            neg_mean = small.tile([P, 1], F32)
            scaled = small.tile([P, HALVES1], F32)
            nc.scalar.activation(
                out=scaled[:], in_=row_sum[:], func=ACT.Identity, scale=-1.0 / D2, accum_out=neg_mean[:],
            )
            stats1[i]["neg_mean"] = neg_mean

        def deviation1(i):
            squares = work.tile([P, D2], F32, bufs=1)
            sq_sum = small.tile([P, 1], F32)
            nc.scalar.activation(
                out=squares[:], in_=u_tiles[i][:], func=ACT.Square,
                bias=stats1[i]["neg_mean"][:], scale=1.0, accum_out=sq_sum[:],
            )
            stats1[i]["sq_sum"] = sq_sum

        def inverse_deviation1(i):
            rstd = small.tile([P, 1], F32)
            nc.scalar.activation(
                out=rstd[:], in_=stats1[i]["sq_sum"][:], func=ACT.Abs_reciprocal_sqrt,
                bias=eps[:], scale=1.0 / D2,
            )
            stats1[i]["rstd"] = rstd

        def normalise1(i):
            z = work.tile([P, D2], F32)
            nc.vector.tensor_scalar(
                out=z[:], in0=u_tiles[i][:], scalar1=stats1[i]["neg_mean"][:], scalar2=stats1[i]["rstd"][:],
                op0=ALU.add, op1=ALU.mult,
            )
            z_tiles[i] = z

        def transpose_z(i, c):
            zt = psum.tile([P, PACK, P], F32, bufs=2)
            for t in range(PACK):
                first = K_PASS * c + P * t
                nc.tensor.transpose(zt[:, t, :], z_tiles[i][:, first : first + P], ident[:])
            z_banks[i, c] = zt

        def gain_shift_relu1(i, c):
            if i not in j_planes:
                planes = work.tile([P, PACK, PASSES2, P], BF16)
                j_planes[i] = planes
            for t in range(PACK):
                j = PACK * c + t
                nc.scalar.activation(
                    out=j_planes[i][:, t, c, :], in_=z_banks[i, c][:, t, :], func=ACT.Relu,
                    scale=gb[:, j : j + 1], bias=gb[:, D2 // P + j : D2 // P + j + 1],
                )

        def regroup_j1(i):
            jg = work.tile([P, PASSES2 * P, PACK], BF16, align_bytes=64)
            regroup(nc.vector.tensor_copy, jg[:], j_planes[i][:].rearrange("p t c n -> p t (c n)"))
            j_grouped[i] = jg

        def quantise_j1(i):
            jc = work.tile([P, PASSES2 * P], U32, align_bytes=64)
            js = work.tile([P, PASSES2 * P], U8, align_bytes=64)
            nc.vector.quantize_mx(
                out=jc[:].bitcast(FP8X4), scales=js[:],
                in_=j_grouped[i][:].rearrange("p n t -> p (n t)"),
            )
            j_codes[i] = jc
            j_scales[i] = js

        def second_product(i):
            acc2 = psum.tile([P, BANK], F32, bufs=1)
            for c in range(PASSES2):
                toks = slice(c * P, (c + 1) * P)
                nc.tensor.matmul_mx(
                    out=acc2[:],
                    lhsT=j_codes[i][:, toks].bitcast(FP8X4),
                    lhsT_scale=j_scales[i][:, toks],
                    rhs=w2_codes[:, c, :].bitcast(FP8X4),
                    rhs_scale=w2_scales[:, c, :],
                    start=(c == 0),
                    stop=(c == PASSES2 - 1),
                )
            w_banks[i] = acc2

        def add_bias2(i):
            w = work.tile([P, D4], F32, bufs=4)
            row_sum2 = small.tile([P, 1], F32)
            nc.vector.scalar_tensor_tensor(
                out=w[:], in0=w_banks[i][:], scalar=1.0, in1=a2_all[:],
                op0=ALU.mult, op1=ALU.add, accum_out=row_sum2[:],
            )
            w_tiles[i] = w
            stats2[i] = {"row_sum": row_sum2}

        def mean2(i):
            neg_mean2 = small.tile([P, 1], F32)
            nc.scalar.activation(
                out=neg_mean2[:], in_=stats2[i]["row_sum"][:], func=ACT.Identity, scale=-1.0 / D4,
            )
            stats2[i]["neg_mean"] = neg_mean2

        def deviation2(i):
            squares2 = work.tile([P, D4], F32, bufs=1)
            sq_sum2 = small.tile([P, 1], F32)
            nc.scalar.activation(
                out=squares2[:], in_=w_tiles[i][:], func=ACT.Square,
                bias=stats2[i]["neg_mean"][:], scale=1.0, accum_out=sq_sum2[:],
            )
            stats2[i]["sq_sum"] = sq_sum2

        def inverse_deviation2(i):
            rstd2 = small.tile([P, 1], F32)
            nc.scalar.activation(
                out=rstd2[:], in_=stats2[i]["sq_sum"][:], func=ACT.Abs_reciprocal_sqrt,
                bias=eps[:], scale=1.0 / D4,
            )
            stats2[i]["rstd"] = rstd2

        x_tiles = {}

        def centre_gain2(i):
            x = work.tile([P, D4], F32, bufs=4)
            nc.vector.scalar_tensor_tensor(
                out=x[:], in0=w_tiles[i][:], scalar=stats2[i]["neg_mean"][:], in1=g2_all[:],
                op0=ALU.add, op1=ALU.mult,
            )
            x_tiles[i] = x

        def scale_shift2(i):
            y = work.tile([P, D4], F32, bufs=4)
            nc.vector.scalar_tensor_tensor(
                out=y[:], in0=x_tiles[i][:], scalar=stats2[i]["rstd"][:], in1=b2_all[:],
                op0=ALU.mult, op1=ALU.add,
            )
            y_tiles[i] = y

        def relu_and_store(i):
            result = work.tile([P, D4], F32, bufs=3)
            if i == TILES - 1:
                nc.vector.tensor_scalar(
                    out=result[:], in0=y_tiles[i][:], scalar1=0.0, scalar2=None, op0=ALU.max,
                )
            else:
                nc.scalar.activation(out=result[:], in_=y_tiles[i][:], func=ACT.Relu)
            nc.sync.dma_start(out=out_rows[i * P : (i + 1) * P, :], in_=result[:])

        last = PASSES1 - 1

        for h in range(HALVES1):
            a1_bank = psum.tile([P, PACK, P], F32, tag="zt", bufs=2)
            for t in range(PACK):
                nc.tensor.matmul(
                    a1_bank[:, t, :], lhsT=a1_raw[:, h, t : t + 1].to_broadcast([P, P]), rhs=ident_bf16[:],
                    start=True, stop=True,
                )
            nc.vector.tensor_copy(out=a1_perm[:, h, :, :], in_=a1_bank[:])
        transpose_query(0)
        for b in range(2):
            query_out_of_psum(0, b)
        for g in range(PASSES1):
            regroup_w1(g)
            if g == 0:
                quantise_query(0)
            if g == last:
                transpose_query(1)
                for b in range(2):
                    query_out_of_psum(1, b)
            if g > 0:
                for h in range(HALVES1):
                    quantise_w1(g - 1, h)
                    first_product_pass(0, h, g - 1)
        for h in range(HALVES1):
            quantise_w1(last, h)
            first_product_pass(0, h, last)
        quantise_query(1)
        for h in range(HALVES1):
            add_bias1(0, h)
        for i in range(Q_BUFS, Q_BUFS + 2):
            load_query(i)

        def run(step, i, *more):
            if 0 <= i < TILES:
                step(i, *more)

        def new_query(i, step, *more):
            if i >= HEAD[step]:
                run(step, i, *more)

        HEAD = {quantise_query: 2, transpose_query: 2, query_out_of_psum: 2}

        def period(i):
            run(load_query, i + 2 + Q_BUFS)
            if i > 0:
                run(add_bias1, i, 1)
            if i > 0:
                run(first_product, i, 0)
            run(gain_shift_relu1, i - 3, 1)
            run(mean1, i - 1)
            run(inverse_deviation2, i - 5)
            run(gain_shift_relu1, i - 3, 0)
            run(centre_gain2, i - 5)
            run(add_bias2, i - 4)
            run(regroup_j1, i - 3)
            if i > 0:
                run(add_bias1, i, 0)
            run(quantise_j1, i - 3)
            new_query(i + 2, transpose_query)
            run(first_product, i + 1, 1)
            run(transpose_z, i - 2, 1)
            run(transpose_z, i - 2, 0)
            run(second_product, i - 3)
            run(deviation1, i - 1)
            run(relu_and_store, i - 6)
            run(mean2, i - 4)
            run(inverse_deviation1, i - 1)
            for b in range(2):
                new_query(i + 2, query_out_of_psum, b)
            run(deviation2, i - 4)
            run(scale_shift2, i - 5)
            run(normalise1, i - 1)
            new_query(i + 2, quantise_query)
            if i == 0:
                regroup_w2(0)
                nc.vector.tensor_copy(out=gb[:, 0 : D2 // P], in_=g1_raw[:].rearrange("p c t -> p (c t)"))
                nc.vector.tensor_copy(out=gb[:, D2 // P : 2 * D2 // P], in_=b1_raw[:].rearrange("p c t -> p (c t)"))
            if i == 1:
                regroup_w2(1)
            if i == 2:
                for c in range(PASSES2):
                    quantise_w2(c)

        for i in range(TILES + 8):
            period(i)
